import numpy as np
import ml_dtypes


def mxq(x, axis, fmt="e4m3"):
    dtype, down = {"e4m3": (ml_dtypes.float8_e4m3fn, 7), "e5m2": (ml_dtypes.float8_e5m2, 14)}[fmt]
    v = np.moveaxis(np.asarray(x, np.float32).astype(ml_dtypes.bfloat16).astype(np.float64), axis, -1)
    blocks = v.reshape(v.shape[:-1] + (-1, 32))
    amax = np.abs(blocks).max(-1, keepdims=True)
    byte = np.maximum(np.where(amax > 0, np.frexp(amax)[1] - 1 + 127, 0) - down, 1)
    scale = np.exp2(byte - 127.0)
    codes = (blocks / scale).astype(np.float32).astype(dtype).astype(np.float64)
    return np.moveaxis((codes * scale).reshape(v.shape), -1, axis)


WIDE = False


def mx_kscale(k):
    if not WIDE:
        return np.ones(k)
    levels = np.array([10, -10, 5, -5, 0])
    a = np.random.permutation(np.resize(levels, k // 512 * 4)).reshape(k // 512, 4)
    idx = np.arange(k)
    return np.exp2(a[idx // 512, idx % 128 // 32])


BF16 = ml_dtypes.bfloat16


def bf(x):
    return np.asarray(x, np.float32).astype(BF16)


def f64(x):
    return np.asarray(x).astype(np.float64)


B, DI, DH, H, DP = 512, 1024, 1024, 4, 1536
HD = DH // H
EPS = 1e-5


def sigmoid(v):
    return 1.0 / (1.0 + np.exp(-v))


def setup_inputs():
    s = mx_kscale(DI)
    d = {"x": bf(np.random.standard_normal((B, DI)) * 1.5 + np.random.standard_normal((B, 1)) * 0.5),
         "h_prev": bf(np.random.standard_normal((B, DH)) * 0.5),
         "c_prev": bf(np.random.standard_normal((B, DH))),
         "n_prev": bf(0.5 + np.abs(np.random.standard_normal((B, DH)))),
         "m_prev": bf(np.random.standard_normal((B, DH))),
         "ln_w": bf((1.0 + 0.1 * np.random.standard_normal(DI)) * s),
         "ln_b": bf(0.2 * np.random.standard_normal(DI) * s)}
    for g in "zifo":
        d["W" + g] = bf(np.random.standard_normal((DI, DH)) / np.sqrt(DI) / s[:, None])
        d["b_" + g] = bf(0.2 * np.random.standard_normal(DH))
        d["R" + g] = bf(np.random.standard_normal((H, HD, HD)) / np.sqrt(HD))
        d["rb_" + g] = bf(0.2 * np.random.standard_normal(DH))
    return d


def reference(x, h_prev, c_prev, n_prev, m_prev, ln_w, ln_b,
              Wz, b_z, Rz, rb_z, Wi, b_i, Ri, rb_i, Wf, b_f, Rf, rb_f, Wo, b_o, Ro, rb_o):
    x = f64(x)
    mu = x.mean(-1, keepdims=True)
    var = x.var(-1, keepdims=True)
    xn = (x - mu) / np.sqrt(var + EPS) * f64(ln_w) + f64(ln_b)
    xq = mxq(xn, 1, "e4m3")
    hr = f64(h_prev).reshape(B, H, HD).transpose(1, 0, 2)

    def gate(W, b, R, rb):
        rec = (hr @ f64(R)).transpose(1, 0, 2).reshape(B, DH)
        return (xq @ mxq(f64(W), 0, "e4m3")) + f64(b) + (rec + f64(rb))

    z_t = gate(Wz, b_z, Rz, rb_z)
    i_t = gate(Wi, b_i, Ri, rb_i)
    f_t = gate(Wf, b_f, Rf, rb_f)
    o_t = gate(Wo, b_o, Ro, rb_o)
    zt = np.tanh(z_t)
    ot = sigmoid(o_t)
    mt = np.maximum(f_t + f64(m_prev), i_t)
    it = np.exp(i_t - mt)
    ft = np.exp(f_t + f64(m_prev) - mt)
    ct = ft * f64(c_prev) + it * zt
    nt = ft * f64(n_prev) + it
    ht = ot * (ct / (nt + 1e-13))
    return (ht, ct, nt, mt)

@@ -1,0 +1,321 @@
+import math
+
+import concourse.mybir as mybir
+from concourse.masks import make_identity
+
+F32 = mybir.dt.float32
+BF16 = mybir.dt.bfloat16
+U32 = mybir.dt.uint32
+U8 = mybir.dt.uint8
+FP8X4 = mybir.dt.float8_e4m3fn_x4
+ALU = mybir.AluOpType
+ACT = mybir.ActivationFunctionType
+
+P = 128
+B, DI, DH, HEADS = 512, 1024, 1024, 4
+HD = DH // HEADS
+ROW_TILES = B // P
+PACK = 4
+K_PASS = P * PACK
+PASSES = DI // K_PASS
+BANK = 512
+HALVES = DH // BANK
+K_TILES = DH // P
+LN_EPS = 1e-5
+N_EPS = 1e-13
+GATES = ("i", "f", "z", "o")
+RAW_AHEAD = 3
+V_COLS = 128
+
+FLOPS = 2 * B * DI * DH * 4 + 2 * B * DH * HD * 4
+
+
+def runs_of_four_out(grouped):
+    return grouped.rearrange("p (c i) t -> p c t i", i=4)
+
+
+def runs_of_four_in(rows):
+    return rows.rearrange("p t (c i) -> p c t i", i=4)
+
+
+def tile_slstmblock_pa_kernel(
+    tc, x, h_prev, c_prev, n_prev, m_prev, ln_w, ln_b,
+    Wz, b_z, Rz, rb_z, Wi, b_i, Ri, rb_i, Wf, b_f, Rf, rb_f, Wo, b_o, Ro, rb_o,
+    out_0, out_1, out_2, out_3,
+):
+    nc = tc.nc
+    weight = {"z": Wz, "i": Wi, "f": Wf, "o": Wo}
+    recurrent = {"z": Rz, "i": Ri, "f": Rf, "o": Ro}
+    biases = {"z": (b_z, rb_z), "i": (b_i, rb_i), "f": (b_f, rb_f), "o": (b_o, rb_o)}
+    h_out, c_out, n_out, m_out = out_0, out_1, out_2, out_3
+
+    def rows_of(dram, t):
+        return dram[t * P : (t + 1) * P, :]
+
+    with (
+        tc.tile_pool(name="const", bufs=1) as const,
+        tc.tile_pool(name="state", bufs=1) as state,
+        tc.tile_pool(name="w_raw", bufs=RAW_AHEAD) as w_raw,
+        tc.tile_pool(name="w_grouped", bufs=2) as w_grouped,
+        tc.tile_pool(name="w_quant", bufs=2 * PASSES) as w_quant,
+        tc.psum_pool(name="psum_mx", bufs=4) as psum_mx,
+    ):
+        ident_f32 = const.tile([P, P], F32)
+        make_identity(nc, ident_f32[:])
+        ident_bf16 = const.tile([P, P], BF16)
+        make_identity(nc, ident_bf16[:])
+        ones = const.tile([P, P], BF16)
+        nc.vector.memset(ones[:], 1.0)
+        minus_half = const.tile([P, 1], F32)
+        nc.vector.memset(minus_half[:], -0.5)
+
+        pre = {g: state.tile([P, ROW_TILES, DH], F32, name="pre_" + g) for g in GATES}
+        x_codes = state.tile([P, PASSES * B], U32, align_bytes=64)
+        x_scales = state.tile([P, PASSES * B], U8, align_bytes=64)
+
+        chunks = [(gate, g) for gate in GATES for g in range(PASSES)]
+        raw_chunk = {}
+        w_codes = {}
+        w_scales = {}
+
+        def start_weight_load(j):
+            gate, g = chunks[j]
+            raw = w_raw.tile([P, PACK, DH], BF16, name="raw")
+            by_pass = weight[gate].rearrange("(g t p) n -> g p t n", t=PACK, p=P)
+            nc.sync.dma_start(out=raw[:], in_=by_pass[g])
+            raw_chunk[j] = raw
+
+        def regroup_and_quantise(rows, codes, scales):
+            grouped = w_grouped.tile([P, DH, PACK], BF16, name="grouped", align_bytes=64)
+            nc.vector.tensor_copy(
+                out=runs_of_four_out(grouped[:, :V_COLS, :]), in_=runs_of_four_in(rows[:, :, :V_COLS])
+            )
+            nc.scalar.copy(
+                out=runs_of_four_out(grouped[:, V_COLS:, :]), in_=runs_of_four_in(rows[:, :, V_COLS:])
+            )
+            for half in range(HALVES):
+                cols = slice(half * BANK, (half + 1) * BANK)
+                nc.vector.quantize_mx(
+                    out=codes[:, cols].bitcast(FP8X4),
+                    scales=scales[:, cols],
+                    in_=grouped[:, cols, :].rearrange("p c t -> p (c t)"),
+                )
+
+        def prepare_weight(j):
+            codes = w_quant.tile([P, DH], U32, name="codes", align_bytes=64)
+            scales = w_quant.tile([P, DH], U8, name="scales", align_bytes=64)
+            regroup_and_quantise(raw_chunk[j][:], codes[:], scales[:])
+            w_codes[chunks[j]] = codes
+            w_scales[chunks[j]] = scales
+            if j + RAW_AHEAD < len(chunks):
+                start_weight_load(j + RAW_AHEAD)
+
+        def add_input_part(gate):
+            for t in range(ROW_TILES):
+                for half in range(HALVES):
+                    cols = slice(half * BANK, (half + 1) * BANK)
+                    acc = psum_mx.tile([P, BANK], F32, name="acc")
+                    for g in range(PASSES):
+                        rows = slice(g * B + t * P, g * B + (t + 1) * P)
+                        nc.tensor.matmul_mx(
+                            out=acc[:],
+                            lhsT=x_codes[:, rows].bitcast(FP8X4),
+                            lhsT_scale=x_scales[:, rows],
+                            rhs=w_codes[(gate, g)][:, cols].bitcast(FP8X4),
+                            rhs_scale=w_scales[(gate, g)][:, cols],
+                            start=(g == 0),
+                            stop=(g == PASSES - 1),
+                        )
+                    nc.vector.tensor_tensor(
+                        out=pre[gate][:, t, cols], in0=acc[:], in1=pre[gate][:, t, cols], op=ALU.add
+                    )
+
+        with (
+            tc.tile_pool(name="early", bufs=1) as early,
+            tc.psum_pool(name="psum_tp", bufs=2) as psum_tp,
+            tc.psum_pool(name="psum_rec", bufs=2) as psum_rec,
+        ):
+            x_sb = early.tile([P, ROW_TILES, DI], BF16)
+            for t in range(ROW_TILES):
+                nc.sync.dma_start(out=x_sb[:, t, :], in_=rows_of(x, t))
+            ln_rows = early.tile([P, P], BF16)
+            nc.vector.memset(ln_rows[:], 0.0)
+            nc.scalar.dma_start(out=ln_rows[0:8, :], in_=ln_w.rearrange("(r c) -> r c", c=P))
+            nc.scalar.dma_start(out=ln_rows[8:16, :], in_=ln_b.rearrange("(r c) -> r c", c=P))
+            bias_rows = early.tile([P, len(GATES), DH], BF16)
+            nc.vector.memset(bias_rows[:], 0.0)
+            for gi, gate in enumerate(GATES):
+                for r, vec in enumerate(biases[gate]):
+                    nc.scalar.dma_start(
+                        out=bias_rows[r : r + 1, gi, :], in_=vec.rearrange("(o n) -> o n", o=1)
+                    )
+            h_sb = early.tile([P, ROW_TILES, DH], BF16)
+            for t in range(ROW_TILES):
+                nc.sync.dma_start(out=h_sb[:, t, :], in_=rows_of(h_prev, t))
+            r_sb = {}
+
+            def load_recurrent(gate):
+                r_sb[gate] = early.tile([P, K_TILES, HD], BF16, name="r_" + gate)
+                nc.sync.dma_start(
+                    out=r_sb[gate][:], in_=recurrent[gate].rearrange("h (kt p) n -> p (h kt) n", p=P)
+                )
+
+            load_recurrent("i")
+            load_recurrent("z")
+            start_weight_load(0)
+            load_recurrent("o")
+            start_weight_load(1)
+            m_sb = early.tile([P, ROW_TILES, DH], BF16)
+            nc.sync.dma_start(out=m_sb[:], in_=m_prev.rearrange("(t p) n -> p t n", p=P))
+            load_recurrent("f")
+            start_weight_load(2)
+
+            stats = early.tile([P, ROW_TILES, 2, 6], F32)
+            mean_var = early.tile([P, ROW_TILES, 2], F32)
+            var_eps = early.tile([P, ROW_TILES], F32)
+            rstd = early.tile([P, ROW_TILES], F32)
+            y = early.tile([P, ROW_TILES, DI], F32)
+            for t in range(ROW_TILES):
+                one = slice(t, t + 1)
+                for s in range(2):
+                    nc.vector.bn_stats(out=stats[:, t, s, :], in_=x_sb[:, t, s * 512 : (s + 1) * 512])
+                nc.vector.bn_aggr(out=mean_var[:, t, :], in_=stats[:, t, :, :].rearrange("p s f -> p (s f)"))
+                nc.gpsimd.tensor_scalar(
+                    out=var_eps[:, one], in0=mean_var[:, t, 1:2], scalar1=LN_EPS, scalar2=None, op0=ALU.add
+                )
+                nc.gpsimd.tensor_tensor(out=rstd[:, one], in0=var_eps[:, one], in1=minus_half[:], op=ALU.pow)
+                nc.gpsimd.tensor_scalar(
+                    out=y[:, t, :], in0=x_sb[:, t, :], scalar1=mean_var[:, t, 0:1], scalar2=rstd[:, one],
+                    op0=ALU.subtract, op1=ALU.mult,
+                )
+
+            ln_ps = psum_tp.tile([P, P], BF16, name="ln_ps", tag="tp")
+            nc.tensor.transpose(ln_ps[:], ln_rows[:], ident_bf16[:])
+            ln_cols = early.tile([P, 16], F32)
+            nc.vector.tensor_copy(out=ln_cols[:], in_=ln_ps[:, 0:16])
+
+            h_t = early.tile([P, K_TILES, B], BF16)
+            for t in range(ROW_TILES):
+                h_ps = psum_tp.tile([P, K_TILES, P], BF16, name="h_ps", tag="tp")
+                for kt in range(K_TILES):
+                    nc.tensor.transpose(h_ps[:, kt, :], h_sb[:, t, kt * P : (kt + 1) * P], ident_bf16[:])
+                nc.scalar.copy(out=h_t[:, :, t * P : (t + 1) * P], in_=h_ps[:])
+
+            bias_sb = early.tile([P, len(GATES), DH], F32)
+            for gi in range(len(GATES)):
+                for half in range(HALVES):
+                    cols = slice(half * BANK, (half + 1) * BANK)
+                    bias_ps = psum_rec.tile([P, BANK], F32, name="bias_ps", tag="rec")
+                    nc.tensor.matmul(out=bias_ps[:], lhsT=ones[:], rhs=bias_rows[:, gi, cols], start=True, stop=True)
+                    nc.scalar.copy(out=bias_sb[:, gi, cols], in_=bias_ps[:])
+
+            def recurrent_part(gate, addend):
+                for t in range(ROW_TILES):
+                    for half in range(HALVES):
+                        cols = slice(half * BANK, (half + 1) * BANK)
+                        rec = psum_rec.tile([P, BANK], F32, name="rec", tag="rec")
+                        for hh in range(BANK // HD):
+                            head = half * (BANK // HD) + hh
+                            for kt in range(HD // P):
+                                k_tile = head * (HD // P) + kt
+                                nc.tensor.matmul(
+                                    out=rec[:, hh * HD : (hh + 1) * HD],
+                                    lhsT=h_t[:, k_tile, t * P : (t + 1) * P],
+                                    rhs=r_sb[gate][:, k_tile, :],
+                                    start=(kt == 0),
+                                    stop=(kt == HD // P - 1),
+                                )
+                        nc.vector.tensor_tensor(
+                            out=pre[gate][:, t, cols], in0=rec[:], in1=addend(t, cols), op=ALU.add
+                        )
+
+            def bias_of(gate):
+                gi = GATES.index(gate)
+                return lambda t, cols: bias_sb[:, gi, cols]
+
+            recurrent_part("i", bias_of("i"))
+            prepare_weight(0)
+            prepare_weight(1)
+
+            xn_t = early.tile([P, PACK, PASSES * B], BF16)
+            for g in range(PASSES):
+                for t4 in range(PACK):
+                    r = g * PACK + t4
+                    y_ps = psum_tp.tile([P, B], F32, name="y_ps", tag="tp")
+                    for t in range(ROW_TILES):
+                        nc.tensor.transpose(y_ps[:, t * P : (t + 1) * P], y[:, t, r * P : (r + 1) * P], ident_f32[:])
+                    nc.scalar.activation(
+                        out=xn_t[:, t4, g * B : (g + 1) * B], in_=y_ps[:], func=ACT.Identity,
+                        bias=ln_cols[:, 8 + r : 9 + r], scale=ln_cols[:, r : r + 1],
+                    )
+            regroup_and_quantise(xn_t[:], x_codes[:], x_scales[:])
+
+            recurrent_part("z", bias_of("z"))
+            recurrent_part("o", bias_of("o"))
+            for t in range(ROW_TILES):
+                nc.gpsimd.tensor_tensor(
+                    out=pre["f"][:, t, :], in0=bias_sb[:, GATES.index("f"), :], in1=m_sb[:, t, :], op=ALU.add
+                )
+            recurrent_part("f", lambda t, cols: pre["f"][:, t, cols])
+
+        with tc.tile_pool(name="late", bufs=1) as late:
+            n_sb = late.tile([P, ROW_TILES, DH], BF16)
+            nc.sync.dma_start(out=n_sb[:], in_=n_prev.rearrange("(t p) n -> p t n", p=P))
+            c_sb = late.tile([P, ROW_TILES, DH], BF16)
+            nc.sync.dma_start(out=c_sb[:], in_=c_prev.rearrange("(t p) n -> p t n", p=P))
+            m_new = late.tile([P, ROW_TILES, DH], F32)
+            n_new = late.tile([P, ROW_TILES, DH], F32)
+            recip = late.tile([P, ROW_TILES, DH], F32)
+
+            add_input_part("i")
+            prepare_weight(2)
+            prepare_weight(3)
+            add_input_part("f")
+
+            for t in range(ROW_TILES):
+                big_i, big_f = pre["i"][:, t, :], pre["f"][:, t, :]
+                nc.vector.tensor_tensor(out=m_new[:, t, :], in0=big_f, in1=big_i, op=ALU.max)
+                nc.sync.dma_start(out=rows_of(m_out, t), in_=m_new[:, t, :])
+                nc.gpsimd.tensor_tensor(out=big_i, in0=big_f, in1=big_i, op=ALU.subtract)
+                nc.scalar.activation(out=big_f, in_=big_i, func=ACT.Exp)
+                nc.scalar.activation(out=big_i, in_=big_i, func=ACT.Exp, scale=-1.0)
+            prepare_weight(4)
+            prepare_weight(5)
+            for t in range(ROW_TILES):
+                exp_minus_d, exp_d = pre["i"][:, t, :], pre["f"][:, t, :]
+                nc.vector.scalar_tensor_tensor(
+                    out=n_new[:, t, :], in0=exp_d, scalar=1.0, in1=n_sb[:, t, :], op0=ALU.min, op1=ALU.mult
+                )
+                nc.vector.scalar_tensor_tensor(
+                    out=n_new[:, t, :], in0=exp_minus_d, scalar=1.0, in1=n_new[:, t, :], op0=ALU.min, op1=ALU.add
+                )
+                nc.sync.dma_start(out=rows_of(n_out, t), in_=n_new[:, t, :])
+                nc.vector.scalar_tensor_tensor(
+                    out=exp_d, in0=exp_d, scalar=1.0, in1=c_sb[:, t, :], op0=ALU.min, op1=ALU.mult
+                )
+            nc.scalar.activation(out=recip[:], in_=n_new[:], func=ACT.Ln, bias=N_EPS)
+
+            add_input_part("z")
+            prepare_weight(6)
+            prepare_weight(7)
+            for t in range(ROW_TILES):
+                exp_minus_d, f_c, z = pre["i"][:, t, :], pre["f"][:, t, :], pre["z"][:, t, :]
+                nc.scalar.activation(out=z, in_=z, func=ACT.Tanh)
+                nc.vector.scalar_tensor_tensor(
+                    out=z, in0=exp_minus_d, scalar=1.0, in1=z, op0=ALU.min, op1=ALU.mult
+                )
+                nc.gpsimd.tensor_tensor(out=f_c, in0=f_c, in1=z, op=ALU.add)
+                nc.sync.dma_start(out=rows_of(c_out, t), in_=f_c)
+                nc.scalar.activation(
+                    out=recip[:, t, :], in_=recip[:, t, :], func=ACT.Exp, bias=math.log(0.5), scale=-1.0
+                )
+                nc.gpsimd.tensor_tensor(out=recip[:, t, :], in0=recip[:, t, :], in1=f_c, op=ALU.mult)
+
+            add_input_part("o")
+            for t in range(ROW_TILES):
+                o = pre["o"][:, t, :]
+                nc.scalar.activation(out=o, in_=o, func=ACT.Tanh, scale=0.5)
+                nc.vector.scalar_tensor_tensor(
+                    out=o, in0=o, scalar=1.0, in1=recip[:, t, :], op0=ALU.add, op1=ALU.mult
+                )
+                nc.sync.dma_start(out=rows_of(h_out, t), in_=o)

@@ -25,7 +25,7 @@ LN_EPS = 1e-5
 N_EPS = 1e-13
 GATES = ("i", "f", "z", "o")
 RAW_AHEAD = 3
-V_COLS = 128
+PIECE = 256
 
 FLOPS = 2 * B * DI * DH * 4 + 2 * B * DH * HD * 4
 
@@ -87,12 +87,11 @@ def tile_slstmblock_pa_kernel(
 
         def regroup_and_quantise(rows, codes, scales):
             grouped = w_grouped.tile([P, DH, PACK], BF16, name="grouped", align_bytes=64)
-            nc.vector.tensor_copy(
-                out=runs_of_four_out(grouped[:, :V_COLS, :]), in_=runs_of_four_in(rows[:, :, :V_COLS])
-            )
-            nc.scalar.copy(
-                out=runs_of_four_out(grouped[:, V_COLS:, :]), in_=runs_of_four_in(rows[:, :, V_COLS:])
-            )
+            for c0 in range(0, DH, PIECE):
+                nc.any.tensor_copy(
+                    out=runs_of_four_out(grouped[:, c0 : c0 + PIECE, :]),
+                    in_=runs_of_four_in(rows[:, :, c0 : c0 + PIECE]),
+                )
             for half in range(HALVES):
                 cols = slice(half * BANK, (half + 1) * BANK)
                 nc.vector.quantize_mx(
@@ -172,21 +171,26 @@ def tile_slstmblock_pa_kernel(
 
             stats = early.tile([P, ROW_TILES, 2, 6], F32)
             mean_var = early.tile([P, ROW_TILES, 2], F32)
+            minus_mean = early.tile([P, ROW_TILES], F32)
             var_eps = early.tile([P, ROW_TILES], F32)
             rstd = early.tile([P, ROW_TILES], F32)
+            shift = early.tile([P, ROW_TILES], F32)
             y = early.tile([P, ROW_TILES, DI], F32)
             for t in range(ROW_TILES):
                 one = slice(t, t + 1)
                 for s in range(2):
                     nc.vector.bn_stats(out=stats[:, t, s, :], in_=x_sb[:, t, s * 512 : (s + 1) * 512])
                 nc.vector.bn_aggr(out=mean_var[:, t, :], in_=stats[:, t, :, :].rearrange("p s f -> p (s f)"))
+                nc.vector.tensor_scalar(
+                    out=minus_mean[:, one], in0=mean_var[:, t, 0:1], scalar1=-1.0, scalar2=None, op0=ALU.mult
+                )
                 nc.gpsimd.tensor_scalar(
                     out=var_eps[:, one], in0=mean_var[:, t, 1:2], scalar1=LN_EPS, scalar2=None, op0=ALU.add
                 )
                 nc.gpsimd.tensor_tensor(out=rstd[:, one], in0=var_eps[:, one], in1=minus_half[:], op=ALU.pow)
-                nc.gpsimd.tensor_scalar(
-                    out=y[:, t, :], in0=x_sb[:, t, :], scalar1=mean_var[:, t, 0:1], scalar2=rstd[:, one],
-                    op0=ALU.subtract, op1=ALU.mult,
+                nc.gpsimd.tensor_tensor(out=shift[:, one], in0=minus_mean[:, one], in1=rstd[:, one], op=ALU.mult)
+                nc.scalar.activation(
+                    out=y[:, t, :], in_=x_sb[:, t, :], func=ACT.Identity, bias=shift[:, one], scale=rstd[:, one]
                 )
 
             ln_ps = psum_tp.tile([P, P], BF16, name="ln_ps", tag="tp")
@@ -199,30 +203,39 @@ def tile_slstmblock_pa_kernel(
                 h_ps = psum_tp.tile([P, K_TILES, P], BF16, name="h_ps", tag="tp")
                 for kt in range(K_TILES):
                     nc.tensor.transpose(h_ps[:, kt, :], h_sb[:, t, kt * P : (kt + 1) * P], ident_bf16[:])
-                nc.scalar.copy(out=h_t[:, :, t * P : (t + 1) * P], in_=h_ps[:])
+                nc.any.tensor_copy(out=h_t[:, :, t * P : (t + 1) * P], in_=h_ps[:])
 
             bias_sb = early.tile([P, len(GATES), DH], F32)
-            for gi in range(len(GATES)):
+            for gate in ("i", "z", "o"):
+                gi = GATES.index(gate)
                 for half in range(HALVES):
                     cols = slice(half * BANK, (half + 1) * BANK)
                     bias_ps = psum_rec.tile([P, BANK], F32, name="bias_ps", tag="rec")
                     nc.tensor.matmul(out=bias_ps[:], lhsT=ones[:], rhs=bias_rows[:, gi, cols], start=True, stop=True)
-                    nc.scalar.copy(out=bias_sb[:, gi, cols], in_=bias_ps[:])
+                    nc.any.tensor_copy(out=bias_sb[:, gi, cols], in_=bias_ps[:])
 
-            def recurrent_part(gate, addend):
+            def recurrent_part(gate, addend, bias_in_psum=False):
                 for t in range(ROW_TILES):
                     for half in range(HALVES):
                         cols = slice(half * BANK, (half + 1) * BANK)
                         rec = psum_rec.tile([P, BANK], F32, name="rec", tag="rec")
                         for hh in range(BANK // HD):
                             head = half * (BANK // HD) + hh
+                            if bias_in_psum:
+                                nc.tensor.matmul(
+                                    out=rec[:, hh * HD : (hh + 1) * HD],
+                                    lhsT=ones[:],
+                                    rhs=bias_rows[:, GATES.index(gate), head * HD : (head + 1) * HD],
+                                    start=True,
+                                    stop=False,
+                                )
                             for kt in range(HD // P):
                                 k_tile = head * (HD // P) + kt
                                 nc.tensor.matmul(
                                     out=rec[:, hh * HD : (hh + 1) * HD],
                                     lhsT=h_t[:, k_tile, t * P : (t + 1) * P],
                                     rhs=r_sb[gate][:, k_tile, :],
-                                    start=(kt == 0),
+                                    start=(kt == 0 and not bias_in_psum),
                                     stop=(kt == HD // P - 1),
                                 )
                         nc.vector.tensor_tensor(
@@ -252,11 +265,7 @@ def tile_slstmblock_pa_kernel(
 
             recurrent_part("z", bias_of("z"))
             recurrent_part("o", bias_of("o"))
-            for t in range(ROW_TILES):
-                nc.gpsimd.tensor_tensor(
-                    out=pre["f"][:, t, :], in0=bias_sb[:, GATES.index("f"), :], in1=m_sb[:, t, :], op=ALU.add
-                )
-            recurrent_part("f", lambda t, cols: pre["f"][:, t, cols])
+            recurrent_part("f", lambda t, cols: m_sb[:, t, cols], bias_in_psum=True)
 
         with tc.tile_pool(name="late", bufs=1) as late:
             n_sb = late.tile([P, ROW_TILES, DH], BF16)
@@ -268,17 +277,19 @@ def tile_slstmblock_pa_kernel(
             recip = late.tile([P, ROW_TILES, DH], F32)
 
             add_input_part("i")
+            for t in range(ROW_TILES):
+                nc.gpsimd.tensor_tensor(out=pre["f"][:, t, :], in0=pre["f"][:, t, :], in1=pre["i"][:, t, :], op=ALU.subtract)
             prepare_weight(2)
             prepare_weight(3)
             add_input_part("f")
-
             for t in range(ROW_TILES):
-                big_i, big_f = pre["i"][:, t, :], pre["f"][:, t, :]
-                nc.vector.tensor_tensor(out=m_new[:, t, :], in0=big_f, in1=big_i, op=ALU.max)
+                big_i, d = pre["i"][:, t, :], pre["f"][:, t, :]
+                nc.vector.scalar_tensor_tensor(
+                    out=m_new[:, t, :], in0=d, scalar=0.0, in1=big_i, op0=ALU.max, op1=ALU.add
+                )
                 nc.sync.dma_start(out=rows_of(m_out, t), in_=m_new[:, t, :])
-                nc.gpsimd.tensor_tensor(out=big_i, in0=big_f, in1=big_i, op=ALU.subtract)
-                nc.scalar.activation(out=big_f, in_=big_i, func=ACT.Exp)
-                nc.scalar.activation(out=big_i, in_=big_i, func=ACT.Exp, scale=-1.0)
+                nc.scalar.activation(out=big_i, in_=d, func=ACT.Exp, scale=-1.0)
+                nc.scalar.activation(out=d, in_=d, func=ACT.Exp)
             prepare_weight(4)
             prepare_weight(5)
             for t in range(ROW_TILES):

@@ -20,7 +20,9 @@ K_PASS = P * PACK
 PASSES = DI // K_PASS
 BANK = 512
 HALVES = DH // BANK
+HEADS_PER_BANK = BANK // HD
 K_TILES = DH // P
+K_TILES_PER_HEAD = HD // P
 LN_EPS = 1e-5
 N_EPS = 1e-13
 GATES = ("i", "f", "z", "o")
@@ -38,6 +40,10 @@ def runs_of_four_in(rows):
     return rows.rearrange("p t (c i) -> p c t i", i=4)
 
 
+def bank_columns(half):
+    return slice(half * BANK, (half + 1) * BANK)
+
+
 def tile_slstmblock_pa_kernel(
     tc, x, h_prev, c_prev, n_prev, m_prev, ln_w, ln_b,
     Wz, b_z, Rz, rb_z, Wi, b_i, Ri, rb_i, Wf, b_f, Rf, rb_f, Wo, b_o, Ro, rb_o,
@@ -52,6 +58,9 @@ def tile_slstmblock_pa_kernel(
     def rows_of(dram, t):
         return dram[t * P : (t + 1) * P, :]
 
+    def by_row_tile(dram):
+        return dram.rearrange("(t p) n -> p t n", p=P)
+
     with (
         tc.tile_pool(name="const", bufs=1) as const,
         tc.tile_pool(name="state", bufs=1) as state,
@@ -59,6 +68,7 @@ def tile_slstmblock_pa_kernel(
         tc.tile_pool(name="w_grouped", bufs=2) as w_grouped,
         tc.tile_pool(name="w_quant", bufs=2 * PASSES) as w_quant,
         tc.psum_pool(name="psum_mx", bufs=4) as psum_mx,
+        tc.psum_pool(name="psum_rec", bufs=2) as psum_rec,
     ):
         ident_f32 = const.tile([P, P], F32)
         make_identity(nc, ident_f32[:])
@@ -72,6 +82,9 @@ def tile_slstmblock_pa_kernel(
         pre = {g: state.tile([P, ROW_TILES, DH], F32, name="pre_" + g) for g in GATES}
         x_codes = state.tile([P, PASSES * B], U32, align_bytes=64)
         x_scales = state.tile([P, PASSES * B], U8, align_bytes=64)
+        h_t = state.tile([P, K_TILES, B], BF16)
+        r_sb = {}
+        bias_sb = {}
 
         chunks = [(gate, g) for gate in GATES for g in range(PASSES)]
         raw_chunk = {}
@@ -93,26 +106,60 @@ def tile_slstmblock_pa_kernel(
                     in_=runs_of_four_in(rows[:, :, c0 : c0 + PIECE]),
                 )
             for half in range(HALVES):
-                cols = slice(half * BANK, (half + 1) * BANK)
+                cols = bank_columns(half)
                 nc.vector.quantize_mx(
                     out=codes[:, cols].bitcast(FP8X4),
                     scales=scales[:, cols],
                     in_=grouped[:, cols, :].rearrange("p c t -> p (c t)"),
                 )
 
-        def prepare_weight(j):
-            codes = w_quant.tile([P, DH], U32, name="codes", align_bytes=64)
-            scales = w_quant.tile([P, DH], U8, name="scales", align_bytes=64)
-            regroup_and_quantise(raw_chunk[j][:], codes[:], scales[:])
-            w_codes[chunks[j]] = codes
-            w_scales[chunks[j]] = scales
-            if j + RAW_AHEAD < len(chunks):
-                start_weight_load(j + RAW_AHEAD)
+        def prepare_weights(gate):
+            for g in range(PASSES):
+                j = chunks.index((gate, g))
+                codes = w_quant.tile([P, DH], U32, name="codes", align_bytes=64)
+                scales = w_quant.tile([P, DH], U8, name="scales", align_bytes=64)
+                regroup_and_quantise(raw_chunk[j][:], codes[:], scales[:])
+                w_codes[(gate, g)] = codes
+                w_scales[(gate, g)] = scales
+                if j + RAW_AHEAD < len(chunks):
+                    start_weight_load(j + RAW_AHEAD)
+
+        def load_recurrent(pool, gate):
+            r_sb[gate] = pool.tile([P, K_TILES, HD], BF16, name="r_" + gate)
+            nc.sync.dma_start(
+                out=r_sb[gate][:], in_=recurrent[gate].rearrange("h (kt p) n -> p (h kt) n", p=P)
+            )
+
+        def recurrent_part(gate, addend, bias_rows=None):
+            for t in range(ROW_TILES):
+                for half in range(HALVES):
+                    rec = psum_rec.tile([P, BANK], F32, name="rec")
+                    for hh in range(HEADS_PER_BANK):
+                        head = half * HEADS_PER_BANK + hh
+                        group = rec[:, hh * HD : (hh + 1) * HD]
+                        if bias_rows is not None:
+                            nc.tensor.matmul(
+                                out=group, lhsT=ones[:], rhs=bias_rows[:, head * HD : (head + 1) * HD],
+                                start=True, stop=False,
+                            )
+                        for kt in range(K_TILES_PER_HEAD):
+                            k_tile = head * K_TILES_PER_HEAD + kt
+                            nc.tensor.matmul(
+                                out=group,
+                                lhsT=h_t[:, k_tile, t * P : (t + 1) * P],
+                                rhs=r_sb[gate][:, k_tile, :],
+                                start=(kt == 0 and bias_rows is None),
+                                stop=(kt == K_TILES_PER_HEAD - 1),
+                            )
+                    cols = bank_columns(half)
+                    nc.vector.tensor_tensor(
+                        out=pre[gate][:, t, cols], in0=rec[:], in1=addend(t, cols), op=ALU.add
+                    )
 
         def add_input_part(gate):
             for t in range(ROW_TILES):
                 for half in range(HALVES):
-                    cols = slice(half * BANK, (half + 1) * BANK)
+                    cols = bank_columns(half)
                     acc = psum_mx.tile([P, BANK], F32, name="acc")
                     for g in range(PASSES):
                         rows = slice(g * B + t * P, g * B + (t + 1) * P)
@@ -132,7 +179,6 @@ def tile_slstmblock_pa_kernel(
         with (
             tc.tile_pool(name="early", bufs=1) as early,
             tc.psum_pool(name="psum_tp", bufs=2) as psum_tp,
-            tc.psum_pool(name="psum_rec", bufs=2) as psum_rec,
         ):
             x_sb = early.tile([P, ROW_TILES, DI], BF16)
             for t in range(ROW_TILES):
@@ -151,23 +197,15 @@ def tile_slstmblock_pa_kernel(
             h_sb = early.tile([P, ROW_TILES, DH], BF16)
             for t in range(ROW_TILES):
                 nc.sync.dma_start(out=h_sb[:, t, :], in_=rows_of(h_prev, t))
-            r_sb = {}
-
-            def load_recurrent(gate):
-                r_sb[gate] = early.tile([P, K_TILES, HD], BF16, name="r_" + gate)
-                nc.sync.dma_start(
-                    out=r_sb[gate][:], in_=recurrent[gate].rearrange("h (kt p) n -> p (h kt) n", p=P)
-                )
-
-            load_recurrent("i")
-            load_recurrent("z")
+            load_recurrent(early, "i")
             start_weight_load(0)
-            load_recurrent("o")
             start_weight_load(1)
             m_sb = early.tile([P, ROW_TILES, DH], BF16)
-            nc.sync.dma_start(out=m_sb[:], in_=m_prev.rearrange("(t p) n -> p t n", p=P))
-            load_recurrent("f")
+            nc.sync.dma_start(out=m_sb[:], in_=by_row_tile(m_prev))
+            load_recurrent(early, "f")
             start_weight_load(2)
+            load_recurrent(state, "z")
+            load_recurrent(state, "o")
 
             stats = early.tile([P, ROW_TILES, 2, 6], F32)
             mean_var = early.tile([P, ROW_TILES, 2], F32)
@@ -198,57 +236,24 @@ def tile_slstmblock_pa_kernel(
             ln_cols = early.tile([P, 16], F32)
             nc.vector.tensor_copy(out=ln_cols[:], in_=ln_ps[:, 0:16])
 
-            h_t = early.tile([P, K_TILES, B], BF16)
             for t in range(ROW_TILES):
                 h_ps = psum_tp.tile([P, K_TILES, P], BF16, name="h_ps", tag="tp")
                 for kt in range(K_TILES):
                     nc.tensor.transpose(h_ps[:, kt, :], h_sb[:, t, kt * P : (kt + 1) * P], ident_bf16[:])
                 nc.any.tensor_copy(out=h_t[:, :, t * P : (t + 1) * P], in_=h_ps[:])
 
-            bias_sb = early.tile([P, len(GATES), DH], F32)
-            for gate in ("i", "z", "o"):
-                gi = GATES.index(gate)
+            for gate, pool in (("i", early), ("z", state), ("o", state)):
+                bias_sb[gate] = pool.tile([P, DH], F32, name="bias_" + gate)
                 for half in range(HALVES):
-                    cols = slice(half * BANK, (half + 1) * BANK)
+                    cols = bank_columns(half)
                     bias_ps = psum_rec.tile([P, BANK], F32, name="bias_ps", tag="rec")
-                    nc.tensor.matmul(out=bias_ps[:], lhsT=ones[:], rhs=bias_rows[:, gi, cols], start=True, stop=True)
-                    nc.any.tensor_copy(out=bias_sb[:, gi, cols], in_=bias_ps[:])
+                    nc.tensor.matmul(
+                        out=bias_ps[:], lhsT=ones[:], rhs=bias_rows[:, GATES.index(gate), cols], start=True, stop=True
+                    )
+                    nc.any.tensor_copy(out=bias_sb[gate][:, cols], in_=bias_ps[:])
 
-            def recurrent_part(gate, addend, bias_in_psum=False):
-                for t in range(ROW_TILES):
-                    for half in range(HALVES):
-                        cols = slice(half * BANK, (half + 1) * BANK)
-                        rec = psum_rec.tile([P, BANK], F32, name="rec", tag="rec")
-                        for hh in range(BANK // HD):
-                            head = half * (BANK // HD) + hh
-                            if bias_in_psum:
-                                nc.tensor.matmul(
-                                    out=rec[:, hh * HD : (hh + 1) * HD],
-                                    lhsT=ones[:],
-                                    rhs=bias_rows[:, GATES.index(gate), head * HD : (head + 1) * HD],
-                                    start=True,
-                                    stop=False,
-                                )
-                            for kt in range(HD // P):
-                                k_tile = head * (HD // P) + kt
-                                nc.tensor.matmul(
-                                    out=rec[:, hh * HD : (hh + 1) * HD],
-                                    lhsT=h_t[:, k_tile, t * P : (t + 1) * P],
-                                    rhs=r_sb[gate][:, k_tile, :],
-                                    start=(kt == 0 and not bias_in_psum),
-                                    stop=(kt == HD // P - 1),
-                                )
-                        nc.vector.tensor_tensor(
-                            out=pre[gate][:, t, cols], in0=rec[:], in1=addend(t, cols), op=ALU.add
-                        )
-
-            def bias_of(gate):
-                gi = GATES.index(gate)
-                return lambda t, cols: bias_sb[:, gi, cols]
-
-            recurrent_part("i", bias_of("i"))
-            prepare_weight(0)
-            prepare_weight(1)
+            recurrent_part("i", lambda t, cols: bias_sb["i"][:, cols])
+            prepare_weights("i")
 
             xn_t = early.tile([P, PACK, PASSES * B], BF16)
             for g in range(PASSES):
@@ -263,15 +268,14 @@ def tile_slstmblock_pa_kernel(
                     )
             regroup_and_quantise(xn_t[:], x_codes[:], x_scales[:])
 
-            recurrent_part("z", bias_of("z"))
-            recurrent_part("o", bias_of("o"))
-            recurrent_part("f", lambda t, cols: m_sb[:, t, cols], bias_in_psum=True)
+            recurrent_part("f", lambda t, cols: m_sb[:, t, cols], bias_rows=bias_rows[:, GATES.index("f"), :])
+            prepare_weights("f")
 
         with tc.tile_pool(name="late", bufs=1) as late:
             n_sb = late.tile([P, ROW_TILES, DH], BF16)
-            nc.sync.dma_start(out=n_sb[:], in_=n_prev.rearrange("(t p) n -> p t n", p=P))
+            nc.sync.dma_start(out=n_sb[:], in_=by_row_tile(n_prev))
             c_sb = late.tile([P, ROW_TILES, DH], BF16)
-            nc.sync.dma_start(out=c_sb[:], in_=c_prev.rearrange("(t p) n -> p t n", p=P))
+            nc.sync.dma_start(out=c_sb[:], in_=by_row_tile(c_prev))
             m_new = late.tile([P, ROW_TILES, DH], F32)
             n_new = late.tile([P, ROW_TILES, DH], F32)
             recip = late.tile([P, ROW_TILES, DH], F32)
@@ -279,8 +283,6 @@ def tile_slstmblock_pa_kernel(
             add_input_part("i")
             for t in range(ROW_TILES):
                 nc.gpsimd.tensor_tensor(out=pre["f"][:, t, :], in0=pre["f"][:, t, :], in1=pre["i"][:, t, :], op=ALU.subtract)
-            prepare_weight(2)
-            prepare_weight(3)
             add_input_part("f")
             for t in range(ROW_TILES):
                 big_i, d = pre["i"][:, t, :], pre["f"][:, t, :]
@@ -290,8 +292,6 @@ def tile_slstmblock_pa_kernel(
                 nc.sync.dma_start(out=rows_of(m_out, t), in_=m_new[:, t, :])
                 nc.scalar.activation(out=big_i, in_=d, func=ACT.Exp, scale=-1.0)
                 nc.scalar.activation(out=d, in_=d, func=ACT.Exp)
-            prepare_weight(4)
-            prepare_weight(5)
             for t in range(ROW_TILES):
                 exp_minus_d, exp_d = pre["i"][:, t, :], pre["f"][:, t, :]
                 nc.vector.scalar_tensor_tensor(
@@ -305,10 +305,14 @@ def tile_slstmblock_pa_kernel(
                     out=exp_d, in0=exp_d, scalar=1.0, in1=c_sb[:, t, :], op0=ALU.min, op1=ALU.mult
                 )
             nc.scalar.activation(out=recip[:], in_=n_new[:], func=ACT.Ln, bias=N_EPS)
+            for t in range(ROW_TILES):
+                nc.scalar.activation(
+                    out=recip[:, t, :], in_=recip[:, t, :], func=ACT.Exp, bias=math.log(0.5), scale=-1.0
+                )
 
+            recurrent_part("z", lambda t, cols: bias_sb["z"][:, cols])
+            prepare_weights("z")
             add_input_part("z")
-            prepare_weight(6)
-            prepare_weight(7)
             for t in range(ROW_TILES):
                 exp_minus_d, f_c, z = pre["i"][:, t, :], pre["f"][:, t, :], pre["z"][:, t, :]
                 nc.scalar.activation(out=z, in_=z, func=ACT.Tanh)
@@ -317,11 +321,10 @@ def tile_slstmblock_pa_kernel(
                 )
                 nc.gpsimd.tensor_tensor(out=f_c, in0=f_c, in1=z, op=ALU.add)
                 nc.sync.dma_start(out=rows_of(c_out, t), in_=f_c)
-                nc.scalar.activation(
-                    out=recip[:, t, :], in_=recip[:, t, :], func=ACT.Exp, bias=math.log(0.5), scale=-1.0
-                )
                 nc.gpsimd.tensor_tensor(out=recip[:, t, :], in0=recip[:, t, :], in1=f_c, op=ALU.mult)
 
+            recurrent_part("o", lambda t, cols: bias_sb["o"][:, cols])
+            prepare_weights("o")
             add_input_part("o")
             for t in range(ROW_TILES):
                 o = pre["o"][:, t, :]

@@ -19,6 +19,7 @@ PACK = 4
 K_PASS = P * PACK
 PASSES = DI // K_PASS
 BANK = 512
+PSUM_BANKS = 8
 HALVES = DH // BANK
 HEADS_PER_BANK = BANK // HD
 K_TILES = DH // P
@@ -67,13 +68,12 @@ def tile_slstmblock_pa_kernel(
         tc.tile_pool(name="w_raw", bufs=RAW_AHEAD) as w_raw,
         tc.tile_pool(name="w_grouped", bufs=2) as w_grouped,
         tc.tile_pool(name="w_quant", bufs=2 * PASSES) as w_quant,
-        tc.psum_pool(name="psum_mx", bufs=4) as psum_mx,
-        tc.psum_pool(name="psum_rec", bufs=2) as psum_rec,
+        tc.psum_pool(name="psum", bufs=PSUM_BANKS) as psum,
     ):
-        ident_f32 = const.tile([P, P], F32)
-        make_identity(nc, ident_f32[:])
         ident_bf16 = const.tile([P, P], BF16)
         make_identity(nc, ident_bf16[:])
+        ident_f32 = const.tile([P, P], F32)
+        make_identity(nc, ident_f32[:])
         ones = const.tile([P, P], BF16)
         nc.vector.memset(ones[:], 1.0)
         minus_half = const.tile([P, 1], F32)
@@ -133,7 +133,7 @@ def tile_slstmblock_pa_kernel(
         def recurrent_part(gate, addend, bias_rows=None):
             for t in range(ROW_TILES):
                 for half in range(HALVES):
-                    rec = psum_rec.tile([P, BANK], F32, name="rec")
+                    rec = psum.tile([P, BANK], F32, name="rec", tag="bank")
                     for hh in range(HEADS_PER_BANK):
                         head = half * HEADS_PER_BANK + hh
                         group = rec[:, hh * HD : (hh + 1) * HD]
@@ -160,7 +160,7 @@ def tile_slstmblock_pa_kernel(
             for t in range(ROW_TILES):
                 for half in range(HALVES):
                     cols = bank_columns(half)
-                    acc = psum_mx.tile([P, BANK], F32, name="acc")
+                    acc = psum.tile([P, BANK], F32, name="acc", tag="bank")
                     for g in range(PASSES):
                         rows = slice(g * B + t * P, g * B + (t + 1) * P)
                         nc.tensor.matmul_mx(
@@ -176,10 +176,7 @@ def tile_slstmblock_pa_kernel(
                         out=pre[gate][:, t, cols], in0=acc[:], in1=pre[gate][:, t, cols], op=ALU.add
                     )
 
-        with (
-            tc.tile_pool(name="early", bufs=1) as early,
-            tc.psum_pool(name="psum_tp", bufs=2) as psum_tp,
-        ):
+        with tc.tile_pool(name="early", bufs=1) as early:
             x_sb = early.tile([P, ROW_TILES, DI], BF16)
             for t in range(ROW_TILES):
                 nc.sync.dma_start(out=x_sb[:, t, :], in_=rows_of(x, t))
@@ -231,22 +228,22 @@ def tile_slstmblock_pa_kernel(
                     out=y[:, t, :], in_=x_sb[:, t, :], func=ACT.Identity, bias=shift[:, one], scale=rstd[:, one]
                 )
 
-            ln_ps = psum_tp.tile([P, P], BF16, name="ln_ps", tag="tp")
+            ln_ps = psum.tile([P, P], BF16, name="ln_ps", tag="bank")
             nc.tensor.transpose(ln_ps[:], ln_rows[:], ident_bf16[:])
             ln_cols = early.tile([P, 16], F32)
             nc.vector.tensor_copy(out=ln_cols[:], in_=ln_ps[:, 0:16])
 
             for t in range(ROW_TILES):
-                h_ps = psum_tp.tile([P, K_TILES, P], BF16, name="h_ps", tag="tp")
+                h_ps = psum.tile([P, K_TILES, P], BF16, name="h_ps", tag="bank")
                 for kt in range(K_TILES):
                     nc.tensor.transpose(h_ps[:, kt, :], h_sb[:, t, kt * P : (kt + 1) * P], ident_bf16[:])
-                nc.any.tensor_copy(out=h_t[:, :, t * P : (t + 1) * P], in_=h_ps[:])
+                nc.scalar.copy(out=h_t[:, :, t * P : (t + 1) * P], in_=h_ps[:])
 
             for gate, pool in (("i", early), ("z", state), ("o", state)):
                 bias_sb[gate] = pool.tile([P, DH], F32, name="bias_" + gate)
                 for half in range(HALVES):
                     cols = bank_columns(half)
-                    bias_ps = psum_rec.tile([P, BANK], F32, name="bias_ps", tag="rec")
+                    bias_ps = psum.tile([P, BANK], F32, name="bias_ps", tag="bank")
                     nc.tensor.matmul(
                         out=bias_ps[:], lhsT=ones[:], rhs=bias_rows[:, GATES.index(gate), cols], start=True, stop=True
                     )
@@ -259,7 +256,7 @@ def tile_slstmblock_pa_kernel(
             for g in range(PASSES):
                 for t4 in range(PACK):
                     r = g * PACK + t4
-                    y_ps = psum_tp.tile([P, B], F32, name="y_ps", tag="tp")
+                    y_ps = psum.tile([P, B], F32, name="y_ps", tag="bank")
                     for t in range(ROW_TILES):
                         nc.tensor.transpose(y_ps[:, t * P : (t + 1) * P], y[:, t, r * P : (r + 1) * P], ident_f32[:])
                     nc.scalar.activation(
@@ -298,12 +295,12 @@ def tile_slstmblock_pa_kernel(
                     out=n_new[:, t, :], in0=exp_d, scalar=1.0, in1=n_sb[:, t, :], op0=ALU.min, op1=ALU.mult
                 )
                 nc.vector.scalar_tensor_tensor(
+                    out=exp_d, in0=exp_d, scalar=1.0, in1=c_sb[:, t, :], op0=ALU.min, op1=ALU.mult
+                )
+                nc.vector.scalar_tensor_tensor(
                     out=n_new[:, t, :], in0=exp_minus_d, scalar=1.0, in1=n_new[:, t, :], op0=ALU.min, op1=ALU.add
                 )
                 nc.sync.dma_start(out=rows_of(n_out, t), in_=n_new[:, t, :])
-                nc.vector.scalar_tensor_tensor(
-                    out=exp_d, in0=exp_d, scalar=1.0, in1=c_sb[:, t, :], op0=ALU.min, op1=ALU.mult
-                )
             nc.scalar.activation(out=recip[:], in_=n_new[:], func=ACT.Ln, bias=N_EPS)
             for t in range(ROW_TILES):
                 nc.scalar.activation(

import math

import concourse.mybir as mybir
from concourse.masks import make_identity

F32 = mybir.dt.float32
BF16 = mybir.dt.bfloat16
U32 = mybir.dt.uint32
U8 = mybir.dt.uint8
FP8X4 = mybir.dt.float8_e4m3fn_x4
ALU = mybir.AluOpType
ACT = mybir.ActivationFunctionType

P = 128
B, DI, DH, HEADS = 512, 1024, 1024, 4
HD = DH // HEADS
ROW_TILES = B // P
PACK = 4
K_PASS = P * PACK
PASSES = DI // K_PASS
BANK = 512
PSUM_BANKS = 8
HALVES = DH // BANK
HEADS_PER_BANK = BANK // HD
K_TILES = DH // P
K_TILES_PER_HEAD = HD // P
LN_EPS = 1e-5
N_EPS = 1e-13
GATES = ("i", "f", "z", "o")
RAW_AHEAD = 3
PIECE = 256

FLOPS = 2 * B * DI * DH * 4 + 2 * B * DH * HD * 4


def runs_of_four_out(grouped):
    return grouped.rearrange("p (c i) t -> p c t i", i=4)


def runs_of_four_in(rows):
    return rows.rearrange("p t (c i) -> p c t i", i=4)


def bank_columns(half):
    return slice(half * BANK, (half + 1) * BANK)


def tile_slstmblock_pa_kernel(
    tc, x, h_prev, c_prev, n_prev, m_prev, ln_w, ln_b,
    Wz, b_z, Rz, rb_z, Wi, b_i, Ri, rb_i, Wf, b_f, Rf, rb_f, Wo, b_o, Ro, rb_o,
    out_0, out_1, out_2, out_3,
):
    nc = tc.nc
    weight = {"z": Wz, "i": Wi, "f": Wf, "o": Wo}
    recurrent = {"z": Rz, "i": Ri, "f": Rf, "o": Ro}
    biases = {"z": (b_z, rb_z), "i": (b_i, rb_i), "f": (b_f, rb_f), "o": (b_o, rb_o)}
    h_out, c_out, n_out, m_out = out_0, out_1, out_2, out_3

    def rows_of(dram, t):
        return dram[t * P : (t + 1) * P, :]

    def by_row_tile(dram):
        return dram.rearrange("(t p) n -> p t n", p=P)

    with (
        tc.tile_pool(name="const", bufs=1) as const,
        tc.tile_pool(name="state", bufs=1) as state,
        tc.tile_pool(name="w_raw", bufs=RAW_AHEAD) as w_raw,
        tc.tile_pool(name="w_grouped", bufs=2) as w_grouped,
        tc.tile_pool(name="w_quant", bufs=2 * PASSES) as w_quant,
        tc.psum_pool(name="psum", bufs=PSUM_BANKS) as psum,
    ):
        ident_bf16 = const.tile([P, P], BF16)
        make_identity(nc, ident_bf16[:])
        ident_f32 = const.tile([P, P], F32)
        make_identity(nc, ident_f32[:])
        ones = const.tile([P, P], BF16)
        nc.vector.memset(ones[:], 1.0)
        minus_half = const.tile([P, 1], F32)
        nc.vector.memset(minus_half[:], -0.5)

        pre = {g: state.tile([P, ROW_TILES, DH], F32, name="pre_" + g) for g in GATES}
        x_codes = state.tile([P, PASSES * B], U32, align_bytes=64)
        x_scales = state.tile([P, PASSES * B], U8, align_bytes=64)
        h_t = state.tile([P, K_TILES, B], BF16)
        r_sb = {}
        bias_sb = {}

        chunks = [(gate, g) for gate in GATES for g in range(PASSES)]
        raw_chunk = {}
        w_codes = {}
        w_scales = {}

        def start_weight_load(j):
            gate, g = chunks[j]
            raw = w_raw.tile([P, PACK, DH], BF16, name="raw")
            by_pass = weight[gate].rearrange("(g t p) n -> g p t n", t=PACK, p=P)
            nc.sync.dma_start(out=raw[:], in_=by_pass[g])
            raw_chunk[j] = raw

        def regroup_and_quantise(rows, codes, scales):
            grouped = w_grouped.tile([P, DH, PACK], BF16, name="grouped", align_bytes=64)
            for c0 in range(0, DH, PIECE):
                nc.any.tensor_copy(
                    out=runs_of_four_out(grouped[:, c0 : c0 + PIECE, :]),
                    in_=runs_of_four_in(rows[:, :, c0 : c0 + PIECE]),
                )
            for half in range(HALVES):
                cols = bank_columns(half)
                nc.vector.quantize_mx(
                    out=codes[:, cols].bitcast(FP8X4),
                    scales=scales[:, cols],
                    in_=grouped[:, cols, :].rearrange("p c t -> p (c t)"),
                )

        def prepare_weights(gate):
            for g in range(PASSES):
                j = chunks.index((gate, g))
                codes = w_quant.tile([P, DH], U32, name="codes", align_bytes=64)
                scales = w_quant.tile([P, DH], U8, name="scales", align_bytes=64)
                regroup_and_quantise(raw_chunk[j][:], codes[:], scales[:])
                w_codes[(gate, g)] = codes
                w_scales[(gate, g)] = scales
                if j + RAW_AHEAD < len(chunks):
                    start_weight_load(j + RAW_AHEAD)

        def load_recurrent(pool, gate):
            r_sb[gate] = pool.tile([P, K_TILES, HD], BF16, name="r_" + gate)
            nc.sync.dma_start(
                out=r_sb[gate][:], in_=recurrent[gate].rearrange("h (kt p) n -> p (h kt) n", p=P)
            )

        def recurrent_part(gate, addend, bias_rows=None):
            for t in range(ROW_TILES):
                for half in range(HALVES):
                    rec = psum.tile([P, BANK], F32, name="rec", tag="bank")
                    for hh in range(HEADS_PER_BANK):
                        head = half * HEADS_PER_BANK + hh
                        group = rec[:, hh * HD : (hh + 1) * HD]
                        if bias_rows is not None:
                            nc.tensor.matmul(
                                out=group, lhsT=ones[:], rhs=bias_rows[:, head * HD : (head + 1) * HD],
                                start=True, stop=False,
                            )
                        for kt in range(K_TILES_PER_HEAD):
                            k_tile = head * K_TILES_PER_HEAD + kt
                            nc.tensor.matmul(
                                out=group,
                                lhsT=h_t[:, k_tile, t * P : (t + 1) * P],
                                rhs=r_sb[gate][:, k_tile, :],
                                start=(kt == 0 and bias_rows is None),
                                stop=(kt == K_TILES_PER_HEAD - 1),
                            )
                    cols = bank_columns(half)
                    nc.vector.tensor_tensor(
                        out=pre[gate][:, t, cols], in0=rec[:], in1=addend(t, cols), op=ALU.add
                    )

        def add_input_part(gate):
            for t in range(ROW_TILES):
                for half in range(HALVES):
                    cols = bank_columns(half)
                    acc = psum.tile([P, BANK], F32, name="acc", tag="bank")
                    for g in range(PASSES):
                        rows = slice(g * B + t * P, g * B + (t + 1) * P)
                        nc.tensor.matmul_mx(
                            out=acc[:],
                            lhsT=x_codes[:, rows].bitcast(FP8X4),
                            lhsT_scale=x_scales[:, rows],
                            rhs=w_codes[(gate, g)][:, cols].bitcast(FP8X4),
                            rhs_scale=w_scales[(gate, g)][:, cols],
                            start=(g == 0),
                            stop=(g == PASSES - 1),
                        )
                    nc.vector.tensor_tensor(
                        out=pre[gate][:, t, cols], in0=acc[:], in1=pre[gate][:, t, cols], op=ALU.add
                    )

        with tc.tile_pool(name="early", bufs=1) as early:
            x_sb = early.tile([P, ROW_TILES, DI], BF16)
            for t in range(ROW_TILES):
                nc.sync.dma_start(out=x_sb[:, t, :], in_=rows_of(x, t))
            ln_rows = early.tile([P, P], BF16)
            nc.vector.memset(ln_rows[:], 0.0)
            nc.scalar.dma_start(out=ln_rows[0:8, :], in_=ln_w.rearrange("(r c) -> r c", c=P))
            nc.scalar.dma_start(out=ln_rows[8:16, :], in_=ln_b.rearrange("(r c) -> r c", c=P))
            bias_rows = early.tile([P, len(GATES), DH], BF16)
            nc.vector.memset(bias_rows[:], 0.0)
            for gi, gate in enumerate(GATES):
                for r, vec in enumerate(biases[gate]):
                    nc.scalar.dma_start(
                        out=bias_rows[r : r + 1, gi, :], in_=vec.rearrange("(o n) -> o n", o=1)
                    )
            h_sb = early.tile([P, ROW_TILES, DH], BF16)
            for t in range(ROW_TILES):
                nc.sync.dma_start(out=h_sb[:, t, :], in_=rows_of(h_prev, t))
            load_recurrent(early, "i")
            start_weight_load(0)
            start_weight_load(1)
            m_sb = early.tile([P, ROW_TILES, DH], BF16)
            nc.sync.dma_start(out=m_sb[:], in_=by_row_tile(m_prev))
            load_recurrent(early, "f")
            start_weight_load(2)
            load_recurrent(state, "z")
            load_recurrent(state, "o")

            stats = early.tile([P, ROW_TILES, 2, 6], F32)
            mean_var = early.tile([P, ROW_TILES, 2], F32)
            minus_mean = early.tile([P, ROW_TILES], F32)
            var_eps = early.tile([P, ROW_TILES], F32)
            rstd = early.tile([P, ROW_TILES], F32)
            shift = early.tile([P, ROW_TILES], F32)
            y = early.tile([P, ROW_TILES, DI], F32)
            for t in range(ROW_TILES):
                one = slice(t, t + 1)
                for s in range(2):
                    nc.vector.bn_stats(out=stats[:, t, s, :], in_=x_sb[:, t, s * 512 : (s + 1) * 512])
                nc.vector.bn_aggr(out=mean_var[:, t, :], in_=stats[:, t, :, :].rearrange("p s f -> p (s f)"))
                nc.vector.tensor_scalar(
                    out=minus_mean[:, one], in0=mean_var[:, t, 0:1], scalar1=-1.0, scalar2=None, op0=ALU.mult
                )
                nc.gpsimd.tensor_scalar(
                    out=var_eps[:, one], in0=mean_var[:, t, 1:2], scalar1=LN_EPS, scalar2=None, op0=ALU.add
                )
                nc.gpsimd.tensor_tensor(out=rstd[:, one], in0=var_eps[:, one], in1=minus_half[:], op=ALU.pow)
                nc.gpsimd.tensor_tensor(out=shift[:, one], in0=minus_mean[:, one], in1=rstd[:, one], op=ALU.mult)
                nc.scalar.activation(
                    out=y[:, t, :], in_=x_sb[:, t, :], func=ACT.Identity, bias=shift[:, one], scale=rstd[:, one]
                )

            ln_ps = psum.tile([P, P], BF16, name="ln_ps", tag="bank")
            nc.tensor.transpose(ln_ps[:], ln_rows[:], ident_bf16[:])
            ln_cols = early.tile([P, 16], F32)
            nc.vector.tensor_copy(out=ln_cols[:], in_=ln_ps[:, 0:16])

            for t in range(ROW_TILES):
                h_ps = psum.tile([P, K_TILES, P], BF16, name="h_ps", tag="bank")
                for kt in range(K_TILES):
                    nc.tensor.transpose(h_ps[:, kt, :], h_sb[:, t, kt * P : (kt + 1) * P], ident_bf16[:])
                nc.scalar.copy(out=h_t[:, :, t * P : (t + 1) * P], in_=h_ps[:])

            for gate, pool in (("i", early), ("z", state), ("o", state)):
                bias_sb[gate] = pool.tile([P, DH], F32, name="bias_" + gate)
                for half in range(HALVES):
                    cols = bank_columns(half)
                    bias_ps = psum.tile([P, BANK], F32, name="bias_ps", tag="bank")
                    nc.tensor.matmul(
                        out=bias_ps[:], lhsT=ones[:], rhs=bias_rows[:, GATES.index(gate), cols], start=True, stop=True
                    )
                    nc.any.tensor_copy(out=bias_sb[gate][:, cols], in_=bias_ps[:])

            recurrent_part("i", lambda t, cols: bias_sb["i"][:, cols])
            prepare_weights("i")

            xn_t = early.tile([P, PACK, PASSES * B], BF16)
            for g in range(PASSES):
                for t4 in range(PACK):
                    r = g * PACK + t4
                    y_ps = psum.tile([P, B], F32, name="y_ps", tag="bank")
                    for t in range(ROW_TILES):
                        nc.tensor.transpose(y_ps[:, t * P : (t + 1) * P], y[:, t, r * P : (r + 1) * P], ident_f32[:])
                    nc.scalar.activation(
                        out=xn_t[:, t4, g * B : (g + 1) * B], in_=y_ps[:], func=ACT.Identity,
                        bias=ln_cols[:, 8 + r : 9 + r], scale=ln_cols[:, r : r + 1],
                    )
            regroup_and_quantise(xn_t[:], x_codes[:], x_scales[:])

            recurrent_part("f", lambda t, cols: m_sb[:, t, cols], bias_rows=bias_rows[:, GATES.index("f"), :])
            prepare_weights("f")

        with tc.tile_pool(name="late", bufs=1) as late:
            n_sb = late.tile([P, ROW_TILES, DH], BF16)
            nc.sync.dma_start(out=n_sb[:], in_=by_row_tile(n_prev))
            c_sb = late.tile([P, ROW_TILES, DH], BF16)
            nc.sync.dma_start(out=c_sb[:], in_=by_row_tile(c_prev))
            m_new = late.tile([P, ROW_TILES, DH], F32)
            n_new = late.tile([P, ROW_TILES, DH], F32)
            recip = late.tile([P, ROW_TILES, DH], F32)

            add_input_part("i")
            for t in range(ROW_TILES):
                nc.gpsimd.tensor_tensor(out=pre["f"][:, t, :], in0=pre["f"][:, t, :], in1=pre["i"][:, t, :], op=ALU.subtract)
            add_input_part("f")
            for t in range(ROW_TILES):
                big_i, d = pre["i"][:, t, :], pre["f"][:, t, :]
                nc.vector.scalar_tensor_tensor(
                    out=m_new[:, t, :], in0=d, scalar=0.0, in1=big_i, op0=ALU.max, op1=ALU.add
                )
                nc.sync.dma_start(out=rows_of(m_out, t), in_=m_new[:, t, :])
                nc.scalar.activation(out=big_i, in_=d, func=ACT.Exp, scale=-1.0)
                nc.scalar.activation(out=d, in_=d, func=ACT.Exp)
            for t in range(ROW_TILES):
                exp_minus_d, exp_d = pre["i"][:, t, :], pre["f"][:, t, :]
                nc.vector.scalar_tensor_tensor(
                    out=n_new[:, t, :], in0=exp_d, scalar=1.0, in1=n_sb[:, t, :], op0=ALU.min, op1=ALU.mult
                )
                nc.vector.scalar_tensor_tensor(
                    out=exp_d, in0=exp_d, scalar=1.0, in1=c_sb[:, t, :], op0=ALU.min, op1=ALU.mult
                )
                nc.vector.scalar_tensor_tensor(
                    out=n_new[:, t, :], in0=exp_minus_d, scalar=1.0, in1=n_new[:, t, :], op0=ALU.min, op1=ALU.add
                )
                nc.sync.dma_start(out=rows_of(n_out, t), in_=n_new[:, t, :])
            nc.scalar.activation(out=recip[:], in_=n_new[:], func=ACT.Ln, bias=N_EPS)
            for t in range(ROW_TILES):
                nc.scalar.activation(
                    out=recip[:, t, :], in_=recip[:, t, :], func=ACT.Exp, bias=math.log(0.5), scale=-1.0
                )

            recurrent_part("z", lambda t, cols: bias_sb["z"][:, cols])
            prepare_weights("z")
            add_input_part("z")
            for t in range(ROW_TILES):
                exp_minus_d, f_c, z = pre["i"][:, t, :], pre["f"][:, t, :], pre["z"][:, t, :]
                nc.scalar.activation(out=z, in_=z, func=ACT.Tanh)
                nc.vector.scalar_tensor_tensor(
                    out=z, in0=exp_minus_d, scalar=1.0, in1=z, op0=ALU.min, op1=ALU.mult
                )
                nc.gpsimd.tensor_tensor(out=f_c, in0=f_c, in1=z, op=ALU.add)
                nc.sync.dma_start(out=rows_of(c_out, t), in_=f_c)
                nc.gpsimd.tensor_tensor(out=recip[:, t, :], in0=recip[:, t, :], in1=f_c, op=ALU.mult)

            recurrent_part("o", lambda t, cols: bias_sb["o"][:, cols])
            prepare_weights("o")
            add_input_part("o")
            for t in range(ROW_TILES):
                o = pre["o"][:, t, :]
                nc.scalar.activation(out=o, in_=o, func=ACT.Tanh, scale=0.5)
                nc.vector.scalar_tensor_tensor(
                    out=o, in0=o, scalar=1.0, in1=recip[:, t, :], op0=ALU.add, op1=ALU.mult
                )
                nc.sync.dma_start(out=rows_of(h_out, t), in_=o)
